import numpy as np
import ml_dtypes


def mxq(x, axis, fmt="e4m3"):
    dtype, down = {"e4m3": (ml_dtypes.float8_e4m3fn, 7), "e5m2": (ml_dtypes.float8_e5m2, 14)}[fmt]
    v = np.moveaxis(np.asarray(x, np.float32).astype(ml_dtypes.bfloat16).astype(np.float64), axis, -1)
    blocks = v.reshape(v.shape[:-1] + (-1, 32))
    amax = np.abs(blocks).max(-1, keepdims=True)
    byte = np.maximum(np.where(amax > 0, np.frexp(amax)[1] - 1 + 127, 0) - down, 1)
    scale = np.exp2(byte - 127.0)
    codes = (blocks / scale).astype(np.float32).astype(dtype).astype(np.float64)
    return np.moveaxis((codes * scale).reshape(v.shape), -1, axis)


WIDE = False


def mx_kscale(k):
    if not WIDE:
        return np.ones(k)
    levels = np.array([10, -10, 5, -5, 0])
    if k % 512:
        return np.exp2(np.random.permutation(np.resize(levels, k // 32))).repeat(32)
    a = np.empty((k // 512, 16))
    for p in range(k // 512):
        a[p, :8] = np.random.permutation(np.resize(levels, 8))
        for g in range(8):
            far = levels[np.abs(levels - a[p, g]) >= 10]
            a[p, g + 8] = far[np.random.randint(len(far))]
    return np.exp2(a.ravel()).repeat(32)


BF16 = ml_dtypes.bfloat16


def bf(x):
    return np.asarray(x, np.float32).astype(BF16)


def f64(x):
    return np.asarray(x).astype(np.float64)


B, N, C, D = 8, 512, 1024, 512
ETA, TAU = 1.0, 1.5


def setup_inputs():
    s, t = mx_kscale(C), mx_kscale(D)
    a = 2.0 * (C / D) ** 0.25 / np.sqrt(C)
    return {"H_t": bf(np.random.standard_normal((B, N, C)) * s),
            "A_stat": bf(np.random.random((N, N))),
            "M_mask": bf(np.random.random((N, N)) - 0.25),
            "Wq": bf(np.random.standard_normal((D, C)) * a * t[:, None] / s),
            "Wk": bf(np.random.standard_normal((D, C)) * a / t[:, None] / s)}


def reference(H_t, A_stat, M_mask, Wq, Wk):
    c = H_t.shape[-1]
    hq = mxq(f64(H_t), 2, "e4m3")
    Q = hq @ mxq(f64(Wq), 1, "e4m3").T
    K = hq @ mxq(f64(Wk), 1, "e4m3").T
    logits = (mxq(Q, 2, "e4m3") @ mxq(K, 2, "e4m3").transpose(0, 2, 1)) / (np.sqrt(c) * TAU)
    logits = 0.5 * (logits + logits.transpose(0, 2, 1))
    n = logits.shape[-1]
    eye = np.eye(n, dtype=bool)
    logits = np.where(eye[None, :, :], -np.inf, logits)
    A_bias = np.where(eye, 0.0, f64(A_stat))
    logits = logits + ETA * A_bias[None, :, :]
    logits = np.where((f64(M_mask) <= 0)[None, :, :], -np.inf, logits)
    e = np.exp(logits - logits.max(-1, keepdims=True))
    return e / e.sum(-1, keepdims=True)

@@ -1,0 +1,296 @@
+from contextlib import ExitStack
+
+import concourse.mybir as mybir
+from concourse.masks import make_identity
+
+F32 = mybir.dt.float32
+BF16 = mybir.dt.bfloat16
+U32 = mybir.dt.uint32
+U8 = mybir.dt.uint8
+FP8X4 = mybir.dt.float8_e4m3fn_x4
+ALU = mybir.AluOpType
+ACT = mybir.ActivationFunctionType
+AX = mybir.AxisListType
+
+B, N, C, D = 8, 512, 1024, 512
+P = 128
+NT = N // P
+FLOPS = 2 * (2 * B * N * C * D) + 2 * B * N * N * D
+SCALE = 0.5 / (1.5 * 32.0)
+BIG = 1.0e38
+Q, K = 0, 1
+
+
+def tile_dynamicgraphattention_t_kernel(tc, H_t, A_stat, M_mask, Wq, Wk, out):
+    nc = tc.nc
+    with ExitStack() as ctx:
+        const = ctx.enter_context(tc.tile_pool(name="const", bufs=1))
+        raw = ctx.enter_context(tc.tile_pool(name="raw", bufs=1))
+        mx = ctx.enter_context(tc.tile_pool(name="mx", bufs=2))
+        work = ctx.enter_context(tc.tile_pool(name="work", bufs=3))
+        small = ctx.enter_context(tc.tile_pool(name="small", bufs=4))
+        psum = ctx.enter_context(tc.psum_pool(name="psum", bufs=1))
+        ctx.enter_context(tc.manual_schedule())
+
+        free = list(range(8))
+        head = {"n": 0}
+
+        def new_bank():
+            k = free[head["n"]]
+            head["n"] += 1
+            return (k, psum.tile([P, 512], F32, name="bank%d" % k, tag="bank%d" % k))
+
+        def copy_out(eng, dst, src):
+            if eng == "V":
+                nc.vector.tensor_copy(out=dst, in_=src)
+            else:
+                nc.scalar.copy(out=dst, in_=src)
+
+        ident = const.tile([P, P], F32, name="ident")
+        make_identity(nc, ident[:])
+        one = const.tile([P, 1], F32, name="one")
+        nc.vector.memset(one[:], 0.0)
+        warm = const.tile([P, 1], F32, name="warm")
+        nc.scalar.activation(out=warm[:], in_=one[:], func=ACT.Exp)
+        pen_diag = const.tile([P, P], BF16, name="pen_diag")
+        nc.vector.tensor_scalar(out=pen_diag[:], in0=ident[:], scalar1=-2.0 * BIG, scalar2=BIG, op0=ALU.mult, op1=ALU.add)
+
+        w_raw = [raw.tile([P, 4, C], BF16, name="w_raw%d" % x) for x in range(2)]
+        h_raw = [raw.tile([P, NT, C], BF16, name="h_raw%d" % b) for b in range(B)]
+        m_sb = const.tile([P, NT, N], BF16, name="m_sb")
+        a_sb = const.tile([P, NT, N], BF16, name="a_sb")
+        w_pen = const.tile([P, NT, N], BF16, name="w_pen")
+        bias = const.tile([P, NT, N], BF16, name="bias")
+        wq_v = Wq.rearrange("(p t) c -> p t c", t=4)
+        wk_v = Wk.rearrange("(p t) c -> p t c", t=4)
+        for t in range(4):
+            nc.sync.dma_start(out=w_raw[Q][:, t, :], in_=wq_v[:, t, :])
+        for j in range(NT):
+            nc.sync.dma_start(out=h_raw[0][:, j, :], in_=H_t[0, j * P:(j + 1) * P, :])
+        for t in range(4):
+            nc.sync.dma_start(out=w_raw[K][:, t, :], in_=wk_v[:, t, :])
+        nc.sync.dma_start(out=h_raw[1][:], in_=H_t[1].rearrange("(j p) c -> p j c", p=P))
+        for b in range(2, B):
+            nc.sync.dma_start(out=h_raw[b][:], in_=H_t[b].rearrange("(j p) c -> p j c", p=P))
+            if b == 2:
+                nc.sync.dma_start(out=m_sb[:], in_=M_mask.rearrange("(i p) m -> p i m", p=P))
+                nc.sync.dma_start(out=a_sb[:], in_=A_stat.rearrange("(i p) m -> p i m", p=P))
+
+        def operand_tiles(tag, bufs):
+            g = mx.tile([P, 4, 2, P, 4], BF16, name=tag + "_g", tag=tag + "_g", bufs=bufs, align_bytes=64)
+            c = mx.tile([P, 4, 2, P], U32, name=tag + "_c", tag=tag + "_c", bufs=bufs, align_bytes=64)
+            s = mx.tile([P, 4, 2, P], U8, name=tag + "_s", tag=tag + "_s", bufs=bufs, align_bytes=64)
+            return g, c, s
+
+        banks = {}
+        w_op = [operand_tiles("w%d" % x, 1) for x in range(2)]
+        h_op = {}
+        qk = {}
+        nlog = {}
+        mins = {}
+        sums = {}
+        probs = {}
+
+        def fill_t(key, src, js):
+            words = src[:].bitcast(F32)
+            for j in js:
+                bank = new_bank()
+                banks[(key, j)] = bank
+                for x in range(4):
+                    g, u = x // 2, x % 2
+                    nc.tensor.transpose(bank[1][:, x * P:(x + 1) * P], words[:, j, 2 * P * g + u:2 * P * (g + 1):2], ident[:])
+
+        def ev_t(key, opnd, js, eng):
+            for j in reversed(js):
+                bank = banks[(key, j)]
+                copy_out(eng, opnd[0][:].bitcast(F32)[:, j], bank[1][:].rearrange("q (g u n) -> q g n u", g=2, u=2))
+                free.append(bank[0])
+
+        def quantise_blocks(opnd, j0, j1):
+            g, c, s = opnd
+            nc.vector.quantize_mx(
+                out=c[:, j0:j1].rearrange("p j g n -> p (j g n)").bitcast(FP8X4),
+                scales=s[:, j0:j1].rearrange("p j g n -> p (j g n)"),
+                in_=g[:, j0:j1].rearrange("p j g n f -> p (j g n f)"),
+            )
+
+        def fill_p(b, x, js):
+            if (b, "g") not in qk:
+                qk[(b, "g")] = mx.tile([P, 2, N, 4], BF16, name="qk_g", tag="qk_g", align_bytes=64)
+                qk[(b, "c")] = mx.tile([P, 2, N], U32, name="qk_c", tag="qk_c", align_bytes=64)
+                qk[(b, "s")] = mx.tile([P, 2, N], U8, name="qk_s", tag="qk_s", align_bytes=64)
+            hc, hs = h_op[b][1], h_op[b][2]
+            wc, ws = w_op[x][1], w_op[x][2]
+            for j in js:
+                bank = new_bank()
+                banks[("p", b, x, j)] = bank
+                for t in range(4):
+                    for g in range(2):
+                        nc.tensor.matmul_mx(
+                            out=bank[1][:, t * P:(t + 1) * P],
+                            lhsT=wc[:, t, g, :].bitcast(FP8X4), lhsT_scale=ws[:, t, g, :],
+                            rhs=hc[:, j, g, :].bitcast(FP8X4), rhs_scale=hs[:, j, g, :],
+                            start=(g == 0), stop=(g == 1),
+                        )
+
+        def ev_p(b, x, js, eng):
+            for j in reversed(js):
+                bank = banks[("p", b, x, j)]
+                copy_out(eng, qk[(b, "g")][:, x, j * P:(j + 1) * P, :], bank[1][:].rearrange("m (t n) -> m n t", t=4))
+                free.append(bank[0])
+
+        def quantise_qk(b, x0, x1):
+            nc.vector.quantize_mx(
+                out=qk[(b, "c")][:, x0:x1, :].rearrange("p x n -> p (x n)").bitcast(FP8X4),
+                scales=qk[(b, "s")][:, x0:x1, :].rearrange("p x n -> p (x n)"),
+                in_=qk[(b, "g")][:, x0:x1].rearrange("p x n t -> p (x n t)"),
+            )
+
+        def fill_s(b, tiles):
+            c, s = qk[(b, "c")], qk[(b, "s")]
+            for i in tiles:
+                bank = new_bank()
+                banks[("s", b, i)] = bank
+                rows = slice(i * P, (i + 1) * P)
+                for x in range(2):
+                    nc.tensor.matmul_mx(
+                        out=bank[1][:],
+                        lhsT=c[:, x, rows].bitcast(FP8X4), lhsT_scale=s[:, x, rows],
+                        rhs=c[:, 1 - x, :].bitcast(FP8X4), rhs_scale=s[:, 1 - x, :],
+                        start=(x == 0), stop=(x == 1),
+                    )
+
+        def make_bias(i):
+            nc.vector.tensor_scalar(out=w_pen[:, i, :], in0=m_sb[:, i, :], scalar1=0.0, scalar2=2.0 * BIG, op0=ALU.is_gt, op1=ALU.mult)
+            nc.vector.scalar_tensor_tensor(out=bias[:, i, :], in0=w_pen[:, i, :], scalar=-BIG, in1=a_sb[:, i, :], op0=ALU.add, op1=ALU.min)
+            blk = bias[:, i, i * P:(i + 1) * P]
+            nc.vector.tensor_tensor(out=blk, in0=blk, in1=pen_diag[:], op=ALU.min)
+
+        def add_bias(b, tiles):
+            if b not in nlog:
+                nlog[b] = work.tile([P, NT, N], F32, name="nlog", tag="nlog")
+                mins[b] = small.tile([P, NT], F32, name="mins", tag="mins")
+            for i in reversed(tiles):
+                bank = banks[("s", b, i)]
+                nc.vector.scalar_tensor_tensor(out=nlog[b][:, i, :], in0=bank[1][:], scalar=-SCALE, in1=bias[:, i, :], op0=ALU.mult, op1=ALU.subtract)
+                free.append(bank[0])
+
+        def row_min(b, i0, i1):
+            nc.vector.tensor_reduce(out=mins[b][:, i0:i1], in_=nlog[b][:, i0:i1, :], axis=AX.X, op=ALU.min)
+
+        def exps(b, tiles):
+            if b not in probs:
+                probs[b] = work.tile([P, NT, N], F32, name="probs", tag="probs")
+                sums[b] = small.tile([P, NT], F32, name="sums", tag="sums")
+            for i in tiles:
+                nc.scalar.activation(out=probs[b][:, i, :], in_=nlog[b][:, i, :], func=ACT.Exp, bias=mins[b][:, i:i + 1], scale=-1.0, accum_out=sums[b][:, i:i + 1])
+
+        recs = {}
+
+        def recip(b, lo, hi):
+            if b not in recs:
+                recs[b] = small.tile([P, NT], F32, name="rs", tag="rs")
+            nc.vector.reciprocal(out=recs[b][:, lo:hi], in_=sums[b][:, lo:hi])
+
+        def normalise(b, tiles, eng):
+            recip(b, tiles[0], tiles[-1] + 1)
+            scale_store(b, tiles, eng)
+
+        def scale_store(b, tiles, eng):
+            rs = recs[b]
+            for i in tiles:
+                e = probs[b][:, i, :]
+                if eng == "V":
+                    nc.vector.tensor_scalar(out=e, in0=e, scalar1=rs[:, i:i + 1], scalar2=None, op0=ALU.mult)
+                else:
+                    nc.scalar.activation(out=e, in_=e, func=ACT.Copy, scale=rs[:, i:i + 1])
+                nc.sync.dma_start(out=out[b, i * P:(i + 1) * P, :], in_=e)
+
+        ALL = (0, 1, 2, 3)
+        for t in range(4):
+            fill_t("wq", w_raw[Q], (t,))
+            ev_t("wq", w_op[Q], (t,), "S")
+            if t > 0:
+                quantise_blocks(w_op[Q], t - 1, t)
+        h_op[0] = operand_tiles("h", 2)
+        for j in range(NT):
+            fill_t("h0", h_raw[0], (j,))
+            ev_t("h0", h_op[0], (j,), "S")
+            if j == 0:
+                quantise_blocks(w_op[Q], 3, 4)
+            else:
+                quantise_blocks(h_op[0], j - 1, j)
+        quantise_blocks(h_op[0], 3, 4)
+        fill_p(0, Q, (0,))
+        fill_t("wk", w_raw[K], ALL)
+        ev_p(0, Q, (0,), "S")
+        ev_t("wk", w_op[K], (0, 1), "S")
+        ev_t("wk", w_op[K], (2, 3), "V")
+        quantise_blocks(w_op[K], 0, 4)
+        fill_p(0, Q, (1, 2, 3))
+        h_op[1] = operand_tiles("h", 2)
+        fill_t("h1", h_raw[1], ALL)
+        ev_p(0, Q, (1, 2, 3), "S")
+        ev_t("h1", h_op[1], (0, 1), "S")
+        ev_t("h1", h_op[1], (2, 3), "V")
+        fill_p(0, K, ALL)
+        quantise_blocks(h_op[1], 0, 4)
+        ev_p(0, K, ALL, "S")
+
+        def has(b):
+            return 0 <= b < B
+
+        for i in range(1, B):
+            if has(i + 1):
+                h_op[i + 1] = operand_tiles("h", 2)
+                fill_t("h%d" % (i + 1), h_raw[i + 1], ALL)
+            if has(i - 2):
+                add_bias(i - 2, ALL)
+            if has(i + 1):
+                ev_t("h%d" % (i + 1), h_op[i + 1], (0, 1, 2), "S")
+                ev_t("h%d" % (i + 1), h_op[i + 1], (3,), "V")
+            fill_p(i, Q, ALL)
+            quantise_qk(i - 1, Q, K + 1)
+            if i == 1:
+                for r in range(NT):
+                    make_bias(r)
+            if has(i - 3):
+                exps(i - 3, ALL)
+            if has(i - 3):
+                recip(i - 3, 0, 4)
+            if has(i - 2):
+                row_min(i - 2, 0, 4)
+            if has(i - 3) and i < B - 1:
+                scale_store(i - 3, ALL, "V")
+            fill_p(i, K, ALL)
+            ev_p(i, Q, ALL, "S")
+            if has(i + 1):
+                quantise_blocks(h_op[i + 1], 0, 4)
+            fill_s(i - 1, ALL)
+            if i < B - 1:
+                ev_p(i, K, ALL, "S")
+        ev_p(B - 1, K, (0, 1), "S")
+        ev_p(B - 1, K, (2, 3), "V")
+        quantise_qk(B - 1, Q, K + 1)
+        exps(B - 3, ALL)
+        scale_store(B - 4, ALL, "S")
+        add_bias(B - 2, ALL)
+        fill_s(B - 1, ALL)
+        recip(B - 3, 0, 4)
+        row_min(B - 2, 0, 4)
+        scale_store(B - 3, ALL, "V")
+        exps(B - 2, ALL)
+        add_bias(B - 1, (0,))
+        for i in range(NT):
+            if i + 1 < NT:
+                add_bias(B - 1, (i + 1,))
+            row_min(B - 1, i, i + 1)
+            exps(B - 1, (i,))
+            if i == 0:
+                recip(B - 2, 0, 4)
+            if i == 1:
+                scale_store(B - 2, ALL, "V")
+        recip(B - 1, 0, 3)
+        scale_store(B - 1, (0, 1, 2), "V")
+        recip(B - 1, 3, 4)
+        scale_store(B - 1, (3,), "V")

@@ -202,6 +202,8 @@ def tile_dynamicgraphattention_t_kernel(tc, H_t, A_stat, M_mask, Wq, Wk, out):
                 e = probs[b][:, i, :]
                 if eng == "V":
                     nc.vector.tensor_scalar(out=e, in0=e, scalar1=rs[:, i:i + 1], scalar2=None, op0=ALU.mult)
+                elif eng == "G":
+                    nc.gpsimd.tensor_scalar(out=e, in0=e, scalar1=rs[:, i:i + 1], scalar2=1.0, op0=ALU.mult, op1=ALU.mult)
                 else:
                     nc.scalar.activation(out=e, in_=e, func=ACT.Copy, scale=rs[:, i:i + 1])
                 nc.sync.dma_start(out=out[b, i * P:(i + 1) * P, :], in_=e)
@@ -261,7 +263,7 @@ def tile_dynamicgraphattention_t_kernel(tc, H_t, A_stat, M_mask, Wq, Wk, out):
             if has(i - 2):
                 row_min(i - 2, 0, 4)
             if has(i - 3) and i < B - 1:
-                scale_store(i - 3, ALL, "V")
+                scale_store(i - 3, ALL, "G")
             fill_p(i, K, ALL)
             ev_p(i, Q, ALL, "S")
             if has(i + 1):

@@ -19,6 +19,8 @@ FLOPS = 2 * (2 * B * N * C * D) + 2 * B * N * N * D
 SCALE = 0.5 / (1.5 * 32.0)
 BIG = 1.0e38
 Q, K = 0, 1
+BANKS = 8
+ALL = (0, 1, 2, 3)
 
 
 def tile_dynamicgraphattention_t_kernel(tc, H_t, A_stat, M_mask, Wq, Wk, out):
@@ -32,13 +34,13 @@ def tile_dynamicgraphattention_t_kernel(tc, H_t, A_stat, M_mask, Wq, Wk, out):
         psum = ctx.enter_context(tc.psum_pool(name="psum", bufs=1))
         ctx.enter_context(tc.manual_schedule())
 
-        free = list(range(8))
-        head = {"n": 0}
+        fills = {"n": 0}
 
         def new_bank():
-            k = free[head["n"]]
-            head["n"] += 1
-            return (k, psum.tile([P, 512], F32, name="bank%d" % k, tag="bank%d" % k))
+            k = fills["n"] % BANKS
+            fills["n"] += 1
+            bank = psum.tile([P, 512], F32, name="bank%d" % k, tag="bank%d" % k)
+            return bank
 
         def copy_out(eng, dst, src):
             if eng == "V":
@@ -52,15 +54,15 @@ def tile_dynamicgraphattention_t_kernel(tc, H_t, A_stat, M_mask, Wq, Wk, out):
         nc.vector.memset(one[:], 0.0)
         warm = const.tile([P, 1], F32, name="warm")
         nc.scalar.activation(out=warm[:], in_=one[:], func=ACT.Exp)
-        pen_diag = const.tile([P, P], BF16, name="pen_diag")
-        nc.vector.tensor_scalar(out=pen_diag[:], in0=ident[:], scalar1=-2.0 * BIG, scalar2=BIG, op0=ALU.mult, op1=ALU.add)
+        pen_diag = const.tile([P, 1, P], BF16, name="pen_diag")
+        nc.vector.tensor_scalar(out=pen_diag[:, 0, :], in0=ident[:], scalar1=-2.0 * BIG, scalar2=BIG, op0=ALU.mult, op1=ALU.add)
 
         w_raw = [raw.tile([P, 4, C], BF16, name="w_raw%d" % x) for x in range(2)]
         h_raw = [raw.tile([P, NT, C], BF16, name="h_raw%d" % b) for b in range(B)]
         m_sb = const.tile([P, NT, N], BF16, name="m_sb")
         a_sb = const.tile([P, NT, N], BF16, name="a_sb")
         w_pen = const.tile([P, NT, N], BF16, name="w_pen")
-        bias = const.tile([P, NT, N], BF16, name="bias")
+        bias = const.tile([P, NT * (N + P)], BF16, name="bias")
         wq_v = Wq.rearrange("(p t) c -> p t c", t=4)
         wk_v = Wk.rearrange("(p t) c -> p t c", t=4)
         for t in range(4):
@@ -69,10 +71,9 @@ def tile_dynamicgraphattention_t_kernel(tc, H_t, A_stat, M_mask, Wq, Wk, out):
             nc.sync.dma_start(out=h_raw[0][:, j, :], in_=H_t[0, j * P:(j + 1) * P, :])
         for t in range(4):
             nc.sync.dma_start(out=w_raw[K][:, t, :], in_=wk_v[:, t, :])
-        nc.sync.dma_start(out=h_raw[1][:], in_=H_t[1].rearrange("(j p) c -> p j c", p=P))
-        for b in range(2, B):
+        for b in range(1, B):
             nc.sync.dma_start(out=h_raw[b][:], in_=H_t[b].rearrange("(j p) c -> p j c", p=P))
-            if b == 2:
+            if b == 1:
                 nc.sync.dma_start(out=m_sb[:], in_=M_mask.rearrange("(i p) m -> p i m", p=P))
                 nc.sync.dma_start(out=a_sb[:], in_=A_stat.rearrange("(i p) m -> p i m", p=P))
 
@@ -89,6 +90,7 @@ def tile_dynamicgraphattention_t_kernel(tc, H_t, A_stat, M_mask, Wq, Wk, out):
         nlog = {}
         mins = {}
         sums = {}
+        recs = {}
         probs = {}
 
         def fill_t(key, src, js):
@@ -96,15 +98,14 @@ def tile_dynamicgraphattention_t_kernel(tc, H_t, A_stat, M_mask, Wq, Wk, out):
             for j in js:
                 bank = new_bank()
                 banks[(key, j)] = bank
-                for x in range(4):
-                    g, u = x // 2, x % 2
-                    nc.tensor.transpose(bank[1][:, x * P:(x + 1) * P], words[:, j, 2 * P * g + u:2 * P * (g + 1):2], ident[:])
+                for g in range(2):
+                    for u in range(2):
+                        x = 2 * g + u
+                        nc.tensor.transpose(bank[:, x * P:(x + 1) * P], words[:, j, 2 * P * g + u:2 * P * (g + 1):2], ident[:])
 
         def ev_t(key, opnd, js, eng):
-            for j in reversed(js):
-                bank = banks[(key, j)]
-                copy_out(eng, opnd[0][:].bitcast(F32)[:, j], bank[1][:].rearrange("q (g u n) -> q g n u", g=2, u=2))
-                free.append(bank[0])
+            for j in js:
+                copy_out(eng, opnd[0][:].bitcast(F32)[:, j], banks[(key, j)][:].rearrange("q (g u n) -> q g n u", g=2, u=2))
 
         def quantise_blocks(opnd, j0, j1):
             g, c, s = opnd
@@ -115,10 +116,12 @@ def tile_dynamicgraphattention_t_kernel(tc, H_t, A_stat, M_mask, Wq, Wk, out):
             )
 
         def fill_p(b, x, js):
-            if (b, "g") not in qk:
-                qk[(b, "g")] = mx.tile([P, 2, N, 4], BF16, name="qk_g", tag="qk_g", align_bytes=64)
-                qk[(b, "c")] = mx.tile([P, 2, N], U32, name="qk_c", tag="qk_c", align_bytes=64)
-                qk[(b, "s")] = mx.tile([P, 2, N], U8, name="qk_s", tag="qk_s", align_bytes=64)
+            if b not in qk:
+                qk[b] = (
+                    mx.tile([P, 2, N, 4], BF16, name="qk_g", tag="qk_g", align_bytes=64),
+                    mx.tile([P, 2, N], U32, name="qk_c", tag="qk_c", align_bytes=64),
+                    mx.tile([P, 2, N], U8, name="qk_s", tag="qk_s", align_bytes=64),
+                )
             hc, hs = h_op[b][1], h_op[b][2]
             wc, ws = w_op[x][1], w_op[x][2]
             for j in js:
@@ -127,53 +130,49 @@ def tile_dynamicgraphattention_t_kernel(tc, H_t, A_stat, M_mask, Wq, Wk, out):
                 for t in range(4):
                     for g in range(2):
                         nc.tensor.matmul_mx(
-                            out=bank[1][:, t * P:(t + 1) * P],
+                            out=bank[:, t * P:(t + 1) * P],
                             lhsT=wc[:, t, g, :].bitcast(FP8X4), lhsT_scale=ws[:, t, g, :],
                             rhs=hc[:, j, g, :].bitcast(FP8X4), rhs_scale=hs[:, j, g, :],
                             start=(g == 0), stop=(g == 1),
                         )
 
         def ev_p(b, x, js, eng):
-            for j in reversed(js):
-                bank = banks[("p", b, x, j)]
-                copy_out(eng, qk[(b, "g")][:, x, j * P:(j + 1) * P, :], bank[1][:].rearrange("m (t n) -> m n t", t=4))
-                free.append(bank[0])
+            for j in js:
+                copy_out(eng, qk[b][0][:, x, j * P:(j + 1) * P, :], banks[("p", b, x, j)][:].rearrange("m (t n) -> m n t", t=4))
 
-        def quantise_qk(b, x0, x1):
-            nc.vector.quantize_mx(
-                out=qk[(b, "c")][:, x0:x1, :].rearrange("p x n -> p (x n)").bitcast(FP8X4),
-                scales=qk[(b, "s")][:, x0:x1, :].rearrange("p x n -> p (x n)"),
-                in_=qk[(b, "g")][:, x0:x1].rearrange("p x n t -> p (x n t)"),
-            )
+        def quantise_qk(b, x):
+            g, c, s = qk[b]
+            nc.vector.quantize_mx(out=c[:, x, :].bitcast(FP8X4), scales=s[:, x, :], in_=g[:, x].rearrange("p n t -> p (n t)"))
 
         def fill_s(b, tiles):
-            c, s = qk[(b, "c")], qk[(b, "s")]
+            c, s = qk[b][1], qk[b][2]
             for i in tiles:
                 bank = new_bank()
                 banks[("s", b, i)] = bank
                 rows = slice(i * P, (i + 1) * P)
                 for x in range(2):
                     nc.tensor.matmul_mx(
-                        out=bank[1][:],
+                        out=bank[:],
                         lhsT=c[:, x, rows].bitcast(FP8X4), lhsT_scale=s[:, x, rows],
                         rhs=c[:, 1 - x, :].bitcast(FP8X4), rhs_scale=s[:, 1 - x, :],
                         start=(x == 0), stop=(x == 1),
                     )
 
-        def make_bias(i):
-            nc.vector.tensor_scalar(out=w_pen[:, i, :], in0=m_sb[:, i, :], scalar1=0.0, scalar2=2.0 * BIG, op0=ALU.is_gt, op1=ALU.mult)
-            nc.vector.scalar_tensor_tensor(out=bias[:, i, :], in0=w_pen[:, i, :], scalar=-BIG, in1=a_sb[:, i, :], op0=ALU.add, op1=ALU.min)
-            blk = bias[:, i, i * P:(i + 1) * P]
-            nc.vector.tensor_tensor(out=blk, in0=blk, in1=pen_diag[:], op=ALU.min)
+        bias_v = bias[:, 0:NT * N].rearrange("p (i m) -> p i m", i=NT)
+
+        def make_bias():
+            nc.vector.tensor_scalar(out=w_pen[:], in0=m_sb[:], scalar1=0.0, scalar2=2.0 * BIG, op0=ALU.is_gt, op1=ALU.mult)
+            nc.vector.tensor_scalar(out=w_pen[:], in0=w_pen[:], scalar1=BIG, scalar2=None, op0=ALU.subtract)
+            nc.vector.tensor_tensor(out=bias_v, in0=w_pen[:], in1=a_sb[:], op=ALU.min)
+            blk = bias[:].rearrange("p (i m) -> p i m", i=NT)[:, :, 0:P]
+            nc.vector.tensor_tensor(out=blk, in0=blk, in1=pen_diag[:].to_broadcast([P, NT, P]), op=ALU.min)
 
         def add_bias(b, tiles):
             if b not in nlog:
                 nlog[b] = work.tile([P, NT, N], F32, name="nlog", tag="nlog")
                 mins[b] = small.tile([P, NT], F32, name="mins", tag="mins")
-            for i in reversed(tiles):
-                bank = banks[("s", b, i)]
-                nc.vector.scalar_tensor_tensor(out=nlog[b][:, i, :], in0=bank[1][:], scalar=-SCALE, in1=bias[:, i, :], op0=ALU.mult, op1=ALU.subtract)
-                free.append(bank[0])
+            for i in tiles:
+                nc.vector.scalar_tensor_tensor(out=nlog[b][:, i, :], in0=banks[("s", b, i)][:], scalar=-SCALE, in1=bias_v[:, i, :], op0=ALU.mult, op1=ALU.subtract)
 
         def row_min(b, i0, i1):
             nc.vector.tensor_reduce(out=mins[b][:, i0:i1], in_=nlog[b][:, i0:i1, :], axis=AX.X, op=ALU.min)
@@ -185,16 +184,10 @@ def tile_dynamicgraphattention_t_kernel(tc, H_t, A_stat, M_mask, Wq, Wk, out):
             for i in tiles:
                 nc.scalar.activation(out=probs[b][:, i, :], in_=nlog[b][:, i, :], func=ACT.Exp, bias=mins[b][:, i:i + 1], scale=-1.0, accum_out=sums[b][:, i:i + 1])
 
-        recs = {}
-
         def recip(b, lo, hi):
             if b not in recs:
                 recs[b] = small.tile([P, NT], F32, name="rs", tag="rs")
             nc.vector.reciprocal(out=recs[b][:, lo:hi], in_=sums[b][:, lo:hi])
-
-        def normalise(b, tiles, eng):
-            recip(b, tiles[0], tiles[-1] + 1)
-            scale_store(b, tiles, eng)
 
         def scale_store(b, tiles, eng):
             rs = recs[b]
@@ -202,13 +195,10 @@ def tile_dynamicgraphattention_t_kernel(tc, H_t, A_stat, M_mask, Wq, Wk, out):
                 e = probs[b][:, i, :]
                 if eng == "V":
                     nc.vector.tensor_scalar(out=e, in0=e, scalar1=rs[:, i:i + 1], scalar2=None, op0=ALU.mult)
-                elif eng == "G":
-                    nc.gpsimd.tensor_scalar(out=e, in0=e, scalar1=rs[:, i:i + 1], scalar2=1.0, op0=ALU.mult, op1=ALU.mult)
                 else:
-                    nc.scalar.activation(out=e, in_=e, func=ACT.Copy, scale=rs[:, i:i + 1])
+                    nc.gpsimd.tensor_scalar(out=e, in0=e, scalar1=rs[:, i:i + 1], scalar2=1.0, op0=ALU.mult, op1=ALU.mult)
                 nc.sync.dma_start(out=out[b, i * P:(i + 1) * P, :], in_=e)
 
-        ALL = (0, 1, 2, 3)
         for t in range(4):
             fill_t("wq", w_raw[Q], (t,))
             ev_t("wq", w_op[Q], (t,), "S")
@@ -223,76 +213,55 @@ def tile_dynamicgraphattention_t_kernel(tc, H_t, A_stat, M_mask, Wq, Wk, out):
             else:
                 quantise_blocks(h_op[0], j - 1, j)
         quantise_blocks(h_op[0], 3, 4)
-        fill_p(0, Q, (0,))
         fill_t("wk", w_raw[K], ALL)
-        ev_p(0, Q, (0,), "S")
         ev_t("wk", w_op[K], (0, 1), "S")
         ev_t("wk", w_op[K], (2, 3), "V")
         quantise_blocks(w_op[K], 0, 4)
-        fill_p(0, Q, (1, 2, 3))
-        h_op[1] = operand_tiles("h", 2)
-        fill_t("h1", h_raw[1], ALL)
-        ev_p(0, Q, (1, 2, 3), "S")
-        ev_t("h1", h_op[1], (0, 1), "S")
-        ev_t("h1", h_op[1], (2, 3), "V")
+        fill_p(0, Q, ALL)
+        ev_p(0, Q, ALL, "S")
         fill_p(0, K, ALL)
-        quantise_blocks(h_op[1], 0, 4)
-        ev_p(0, K, ALL, "S")
-
-        def has(b):
-            return 0 <= b < B
+        quantise_qk(0, Q)
+        make_bias()
 
         for i in range(1, B):
-            if has(i + 1):
-                h_op[i + 1] = operand_tiles("h", 2)
-                fill_t("h%d" % (i + 1), h_raw[i + 1], ALL)
-            if has(i - 2):
-                add_bias(i - 2, ALL)
-            if has(i + 1):
-                ev_t("h%d" % (i + 1), h_op[i + 1], (0, 1, 2), "S")
-                ev_t("h%d" % (i + 1), h_op[i + 1], (3,), "V")
-            fill_p(i, Q, ALL)
-            quantise_qk(i - 1, Q, K + 1)
-            if i == 1:
-                for r in range(NT):
-                    make_bias(r)
-            if has(i - 3):
-                exps(i - 3, ALL)
-            if has(i - 3):
-                recip(i - 3, 0, 4)
-            if has(i - 2):
-                row_min(i - 2, 0, 4)
-            if has(i - 3) and i < B - 1:
-                scale_store(i - 3, ALL, "G")
-            fill_p(i, K, ALL)
-            ev_p(i, Q, ALL, "S")
-            if has(i + 1):
-                quantise_blocks(h_op[i + 1], 0, 4)
+            h_op[i] = operand_tiles("h", 2)
+            fill_t("h%d" % i, h_raw[i], ALL)
+            ev_p(i - 1, K, ALL, "S")
+            quantise_qk(i - 1, K)
             fill_s(i - 1, ALL)
-            if i < B - 1:
-                ev_p(i, K, ALL, "S")
-        ev_p(B - 1, K, (0, 1), "S")
-        ev_p(B - 1, K, (2, 3), "V")
-        quantise_qk(B - 1, Q, K + 1)
-        exps(B - 3, ALL)
-        scale_store(B - 4, ALL, "S")
-        add_bias(B - 2, ALL)
-        fill_s(B - 1, ALL)
-        recip(B - 3, 0, 4)
-        row_min(B - 2, 0, 4)
-        scale_store(B - 3, ALL, "V")
-        exps(B - 2, ALL)
-        add_bias(B - 1, (0,))
+            ev_t("h%d" % i, h_op[i], (0, 1, 2), "S")
+            ev_t("h%d" % i, h_op[i], (3,), "V")
+            quantise_blocks(h_op[i], 0, 2)
+            add_bias(i - 1, (0,))
+            quantise_blocks(h_op[i], 2, 4)
+            fill_p(i, Q, ALL)
+            add_bias(i - 1, (1, 2, 3))
+            fill_p(i, K, ALL)
+            row_min(i - 1, 0, NT)
+            if i >= 2:
+                exps(i - 2, ALL)
+            ev_p(i, Q, ALL, "S")
+            quantise_qk(i, Q)
+            if i >= 2:
+                recip(i - 2, 0, NT)
+                scale_store(i - 2, ALL, "G")
+        b = B - 1
+        ev_p(b, K, (0, 1, 2), "S")
+        ev_p(b, K, (3,), "V")
+        quantise_qk(b, K)
+        fill_s(b, ALL)
+        exps(b - 1, ALL)
         for i in range(NT):
-            if i + 1 < NT:
-                add_bias(B - 1, (i + 1,))
-            row_min(B - 1, i, i + 1)
-            exps(B - 1, (i,))
-            if i == 0:
-                recip(B - 2, 0, 4)
+            add_bias(b, (i,))
+            if i > 0:
+                row_min(b, i - 1, i)
+                exps(b, (i - 1,))
             if i == 1:
-                scale_store(B - 2, ALL, "V")
-        recip(B - 1, 0, 3)
-        scale_store(B - 1, (0, 1, 2), "V")
-        recip(B - 1, 3, 4)
-        scale_store(B - 1, (3,), "V")
+                recip(b - 1, 0, NT)
+                scale_store(b - 1, ALL, "G")
+        row_min(b, 3, 4)
+        exps(b, (3,))
+        recip(b, 0, 3)
+        scale_store(b, (0, 1, 2), "V")
+        recip(b, 3, 4)
+        scale_store(b, (3,), "V")

@@ -217,37 +217,42 @@ def tile_dynamicgraphattention_t_kernel(tc, H_t, A_stat, M_mask, Wq, Wk, out):
         ev_t("wk", w_op[K], (0, 1), "S")
         ev_t("wk", w_op[K], (2, 3), "V")
         quantise_blocks(w_op[K], 0, 4)
+        h_op[1] = operand_tiles("h", 2)
+        fill_t("h1", h_raw[1], ALL)
+        ev_t("h1", h_op[1], (1, 0), "S")
+        ev_t("h1", h_op[1], (3, 2), "V")
+        quantise_blocks(h_op[1], 0, 4)
         fill_p(0, Q, ALL)
         ev_p(0, Q, ALL, "S")
         fill_p(0, K, ALL)
-        quantise_qk(0, Q)
         make_bias()
+        quantise_qk(0, Q)
 
         for i in range(1, B):
-            h_op[i] = operand_tiles("h", 2)
-            fill_t("h%d" % i, h_raw[i], ALL)
+            if i + 1 < B:
+                fill_t("h%d" % (i + 1), h_raw[i + 1], ALL)
             ev_p(i - 1, K, ALL, "S")
             quantise_qk(i - 1, K)
-            fill_s(i - 1, ALL)
-            ev_t("h%d" % i, h_op[i], (0, 1, 2), "S")
-            ev_t("h%d" % i, h_op[i], (3,), "V")
-            quantise_blocks(h_op[i], 0, 2)
-            add_bias(i - 1, (0,))
-            quantise_blocks(h_op[i], 2, 4)
             fill_p(i, Q, ALL)
-            add_bias(i - 1, (1, 2, 3))
+            if i + 1 < B:
+                h_op[i + 1] = operand_tiles("h", 2)
+                ev_t("h%d" % (i + 1), h_op[i + 1], (1, 0), "S")
+                ev_t("h%d" % (i + 1), h_op[i + 1], (3, 2), "V")
+                quantise_blocks(h_op[i + 1], 0, 4)
+            fill_s(i - 1, ALL)
+            ev_p(i, Q, ALL, "S")
             fill_p(i, K, ALL)
-            row_min(i - 1, 0, NT)
             if i >= 2:
                 exps(i - 2, ALL)
-            ev_p(i, Q, ALL, "S")
+            add_bias(i - 1, ALL)
             quantise_qk(i, Q)
+            row_min(i - 1, 0, NT)
             if i >= 2:
                 recip(i - 2, 0, NT)
                 scale_store(i - 2, ALL, "G")
         b = B - 1
-        ev_p(b, K, (0, 1, 2), "S")
-        ev_p(b, K, (3,), "V")
+        ev_p(b, K, (0, 2), "S")
+        ev_p(b, K, (1, 3), "V")
         quantise_qk(b, K)
         fill_s(b, ALL)
         exps(b - 1, ALL)

@@ -30,6 +30,7 @@ def tile_dynamicgraphattention_t_kernel(tc, H_t, A_stat, M_mask, Wq, Wk, out):
         raw = ctx.enter_context(tc.tile_pool(name="raw", bufs=1))
         mx = ctx.enter_context(tc.tile_pool(name="mx", bufs=2))
         work = ctx.enter_context(tc.tile_pool(name="work", bufs=3))
+        perm = ctx.enter_context(tc.tile_pool(name="perm", bufs=2))
         small = ctx.enter_context(tc.tile_pool(name="small", bufs=4))
         psum = ctx.enter_context(tc.psum_pool(name="psum", bufs=1))
         ctx.enter_context(tc.manual_schedule())
@@ -103,6 +104,23 @@ def tile_dynamicgraphattention_t_kernel(tc, H_t, A_stat, M_mask, Wq, Wk, out):
                         x = 2 * g + u
                         nc.tensor.transpose(bank[:, x * P:(x + 1) * P], words[:, j, 2 * P * g + u:2 * P * (g + 1):2], ident[:])
 
+        def split_words(src):
+            both = []
+            for j in (0, 2):
+                dst = perm.tile([P, 2, 2, 512 // 2], F32, name="half%d" % j, tag="half%d" % j)
+                nc.vector.tensor_copy(out=dst[:].rearrange("p u j w -> p u (j w)"), in_=src[:, j:j + 2, :].rearrange("p j c -> p (j c)").bitcast(F32).rearrange("p (w u) -> p u w", u=2))
+                both.append(dst)
+            return both
+
+        def fill_t2(key, both):
+            for j in range(NT):
+                bank = new_bank()
+                banks[(key, j)] = bank
+                for g in range(2):
+                    for u in range(2):
+                        x = 2 * g + u
+                        nc.tensor.transpose(bank[:, x * P:(x + 1) * P], both[j // 2][:, u, j % 2, g * P:(g + 1) * P], ident[:])
+
         def ev_t(key, opnd, js, eng):
             for j in js:
                 copy_out(eng, opnd[0][:].bitcast(F32)[:, j], banks[(key, j)][:].rearrange("q (g u n) -> q g n u", g=2, u=2))
@@ -169,7 +187,7 @@ def tile_dynamicgraphattention_t_kernel(tc, H_t, A_stat, M_mask, Wq, Wk, out):
 
         def add_bias(b, tiles):
             if b not in nlog:
-                nlog[b] = work.tile([P, NT, N], F32, name="nlog", tag="nlog")
+                nlog[b] = work.tile([P, NT, N], F32, name="nlog", tag="nlog", bufs=2)
                 mins[b] = small.tile([P, NT], F32, name="mins", tag="mins")
             for i in tiles:
                 nc.vector.scalar_tensor_tensor(out=nlog[b][:, i, :], in0=banks[("s", b, i)][:], scalar=-SCALE, in1=bias_v[:, i, :], op0=ALU.mult, op1=ALU.subtract)
@@ -213,15 +231,17 @@ def tile_dynamicgraphattention_t_kernel(tc, H_t, A_stat, M_mask, Wq, Wk, out):
             else:
                 quantise_blocks(h_op[0], j - 1, j)
         quantise_blocks(h_op[0], 3, 4)
-        fill_t("wk", w_raw[K], ALL)
+        fill_t2("wk", split_words(w_raw[K]))
         ev_t("wk", w_op[K], (0, 1), "S")
-        ev_t("wk", w_op[K], (2, 3), "V")
+        ev_t("wk", w_op[K], (3, 2), "V")
         quantise_blocks(w_op[K], 0, 4)
         h_op[1] = operand_tiles("h", 2)
-        fill_t("h1", h_raw[1], ALL)
+        split = {1: split_words(h_raw[1])}
+        fill_t2("h1", split[1])
         ev_t("h1", h_op[1], (1, 0), "S")
         ev_t("h1", h_op[1], (3, 2), "V")
         quantise_blocks(h_op[1], 0, 4)
+        split[2] = split_words(h_raw[2])
         fill_p(0, Q, ALL)
         ev_p(0, Q, ALL, "S")
         fill_p(0, K, ALL)
@@ -230,15 +250,18 @@ def tile_dynamicgraphattention_t_kernel(tc, H_t, A_stat, M_mask, Wq, Wk, out):
 
         for i in range(1, B):
             if i + 1 < B:
-                fill_t("h%d" % (i + 1), h_raw[i + 1], ALL)
+                fill_t2("h%d" % (i + 1), split[i + 1])
+            if i + 2 < B:
+                split[i + 2] = split_words(h_raw[i + 2])
             ev_p(i - 1, K, ALL, "S")
             quantise_qk(i - 1, K)
             fill_p(i, Q, ALL)
             if i + 1 < B:
                 h_op[i + 1] = operand_tiles("h", 2)
-                ev_t("h%d" % (i + 1), h_op[i + 1], (1, 0), "S")
-                ev_t("h%d" % (i + 1), h_op[i + 1], (3, 2), "V")
-                quantise_blocks(h_op[i + 1], 0, 4)
+                ev_t("h%d" % (i + 1), h_op[i + 1], (0, 1, 2), "S")
+                ev_t("h%d" % (i + 1), h_op[i + 1], (3,), "V")
+                quantise_blocks(h_op[i + 1], 0, 2)
+                quantise_blocks(h_op[i + 1], 2, 4)
             fill_s(i - 1, ALL)
             ev_p(i, Q, ALL, "S")
             fill_p(i, K, ALL)

@@ -74,7 +74,7 @@ def tile_dynamicgraphattention_t_kernel(tc, H_t, A_stat, M_mask, Wq, Wk, out):
             nc.sync.dma_start(out=w_raw[K][:, t, :], in_=wk_v[:, t, :])
         for b in range(1, B):
             nc.sync.dma_start(out=h_raw[b][:], in_=H_t[b].rearrange("(j p) c -> p j c", p=P))
-            if b == 1:
+            if b == 2:
                 nc.sync.dma_start(out=m_sb[:], in_=M_mask.rearrange("(i p) m -> p i m", p=P))
                 nc.sync.dma_start(out=a_sb[:], in_=A_stat.rearrange("(i p) m -> p i m", p=P))
 
@@ -158,9 +158,10 @@ def tile_dynamicgraphattention_t_kernel(tc, H_t, A_stat, M_mask, Wq, Wk, out):
             for j in js:
                 copy_out(eng, qk[b][0][:, x, j * P:(j + 1) * P, :], banks[("p", b, x, j)][:].rearrange("m (t n) -> m n t", t=4))
 
-        def quantise_qk(b, x):
+        def quantise_qk(b, x, j0=0, j1=NT):
             g, c, s = qk[b]
-            nc.vector.quantize_mx(out=c[:, x, :].bitcast(FP8X4), scales=s[:, x, :], in_=g[:, x].rearrange("p n t -> p (n t)"))
+            n = slice(j0 * P, j1 * P)
+            nc.vector.quantize_mx(out=c[:, x, n].bitcast(FP8X4), scales=s[:, x, n], in_=g[:, x, n].rearrange("p n t -> p (n t)"))
 
         def fill_s(b, tiles):
             c, s = qk[b][1], qk[b][2]
@@ -231,22 +232,21 @@ def tile_dynamicgraphattention_t_kernel(tc, H_t, A_stat, M_mask, Wq, Wk, out):
             else:
                 quantise_blocks(h_op[0], j - 1, j)
         quantise_blocks(h_op[0], 3, 4)
-        fill_t2("wk", split_words(w_raw[K]))
+        fill_t("wk", w_raw[K], ALL)
         ev_t("wk", w_op[K], (0, 1), "S")
         ev_t("wk", w_op[K], (3, 2), "V")
         quantise_blocks(w_op[K], 0, 4)
+        fill_p(0, Q, ALL)
         h_op[1] = operand_tiles("h", 2)
-        split = {1: split_words(h_raw[1])}
-        fill_t2("h1", split[1])
+        fill_t("h1", h_raw[1], ALL)
+        ev_p(0, Q, ALL, "S")
         ev_t("h1", h_op[1], (1, 0), "S")
         ev_t("h1", h_op[1], (3, 2), "V")
         quantise_blocks(h_op[1], 0, 4)
-        split[2] = split_words(h_raw[2])
-        fill_p(0, Q, ALL)
-        ev_p(0, Q, ALL, "S")
+        split = {2: split_words(h_raw[2])}
         fill_p(0, K, ALL)
-        make_bias()
         quantise_qk(0, Q)
+        make_bias()
 
         for i in range(1, B):
             if i + 1 < B:
@@ -269,14 +269,15 @@ def tile_dynamicgraphattention_t_kernel(tc, H_t, A_stat, M_mask, Wq, Wk, out):
                 exps(i - 2, ALL)
             add_bias(i - 1, ALL)
             quantise_qk(i, Q)
-            row_min(i - 1, 0, NT)
+            row_min(i - 1, 0, NT if i + 1 < B else 2)
             if i >= 2:
                 recip(i - 2, 0, NT)
                 scale_store(i - 2, ALL, "G")
         b = B - 1
-        ev_p(b, K, (0, 2), "S")
-        ev_p(b, K, (1, 3), "V")
-        quantise_qk(b, K)
+        ev_p(b, K, ALL, "S")
+        quantise_qk(b, K, 0, 2)
+        quantise_qk(b, K, 2, 4)
+        row_min(b - 1, 2, NT)
         fill_s(b, ALL)
         exps(b - 1, ALL)
         for i in range(NT):

@@ -21,6 +21,7 @@ BIG = 1.0e38
 Q, K = 0, 1
 BANKS = 8
 ALL = (0, 1, 2, 3)
+PARTED = 3
 
 
 def tile_dynamicgraphattention_t_kernel(tc, H_t, A_stat, M_mask, Wq, Wk, out):
@@ -104,22 +105,19 @@ def tile_dynamicgraphattention_t_kernel(tc, H_t, A_stat, M_mask, Wq, Wk, out):
                         x = 2 * g + u
                         nc.tensor.transpose(bank[:, x * P:(x + 1) * P], words[:, j, 2 * P * g + u:2 * P * (g + 1):2], ident[:])
 
-        def split_words(src):
-            both = []
-            for j in (0, 2):
-                dst = perm.tile([P, 2, 2, 512 // 2], F32, name="half%d" % j, tag="half%d" % j)
-                nc.vector.tensor_copy(out=dst[:].rearrange("p u j w -> p u (j w)"), in_=src[:, j:j + 2, :].rearrange("p j c -> p (j c)").bitcast(F32).rearrange("p (w u) -> p u w", u=2))
-                both.append(dst)
-            return both
+        def part_words(src):
+            dst = perm.tile([P, 2, PARTED, 2 * P], F32, name="parted", tag="parted")
+            nc.vector.tensor_copy(out=dst[:].rearrange("p u j w -> p u (j w)"), in_=src[:, 0:PARTED, :].rearrange("p j c -> p (j c)").bitcast(F32).rearrange("p (w u) -> p u w", u=2))
+            return dst
 
-        def fill_t2(key, both):
-            for j in range(NT):
+        def fill_parted(key, dst, js):
+            for j in js:
                 bank = new_bank()
                 banks[(key, j)] = bank
                 for g in range(2):
                     for u in range(2):
                         x = 2 * g + u
-                        nc.tensor.transpose(bank[:, x * P:(x + 1) * P], both[j // 2][:, u, j % 2, g * P:(g + 1) * P], ident[:])
+                        nc.tensor.transpose(bank[:, x * P:(x + 1) * P], dst[:, u, j, g * P:(g + 1) * P], ident[:])
 
         def ev_t(key, opnd, js, eng):
             for j in js:
@@ -243,36 +241,46 @@ def tile_dynamicgraphattention_t_kernel(tc, H_t, A_stat, M_mask, Wq, Wk, out):
         ev_t("h1", h_op[1], (1, 0), "S")
         ev_t("h1", h_op[1], (3, 2), "V")
         quantise_blocks(h_op[1], 0, 4)
-        split = {2: split_words(h_raw[2])}
+        parted = {}
         fill_p(0, K, ALL)
         quantise_qk(0, Q)
         make_bias()
 
         for i in range(1, B):
-            if i + 1 < B:
-                fill_t2("h%d" % (i + 1), split[i + 1])
-            if i + 2 < B:
-                split[i + 2] = split_words(h_raw[i + 2])
+            h = i + 1
+            key = "h%d" % h
+            if h in parted:
+                fill_parted(key, parted[h], range(PARTED))
+                fill_t(key, h_raw[h], range(PARTED, NT))
+            elif h < B:
+                fill_t(key, h_raw[h], ALL)
             ev_p(i - 1, K, ALL, "S")
             quantise_qk(i - 1, K)
             fill_p(i, Q, ALL)
-            if i + 1 < B:
-                h_op[i + 1] = operand_tiles("h", 2)
-                ev_t("h%d" % (i + 1), h_op[i + 1], (0, 1, 2), "S")
-                ev_t("h%d" % (i + 1), h_op[i + 1], (3,), "V")
-                quantise_blocks(h_op[i + 1], 0, 2)
-                quantise_blocks(h_op[i + 1], 2, 4)
+            if h < B:
+                h_op[h] = operand_tiles("h", 2)
+                ev_t(key, h_op[h], (1, 0), "S")
+                ev_t(key, h_op[h], (3, 2), "V")
+                if h + 1 < B:
+                    parted[h + 1] = part_words(h_raw[h + 1])
+                quantise_blocks(h_op[h], 0, 2)
             fill_s(i - 1, ALL)
             ev_p(i, Q, ALL, "S")
             fill_p(i, K, ALL)
             if i >= 2:
                 exps(i - 2, ALL)
             add_bias(i - 1, ALL)
-            quantise_qk(i, Q)
-            row_min(i - 1, 0, NT if i + 1 < B else 2)
+            if h < B:
+                quantise_blocks(h_op[h], 2, 4)
+                row_min(i - 1, 0, NT)
+            else:
+                quantise_qk(i, Q)
+                row_min(i - 1, 0, 2)
             if i >= 2:
                 recip(i - 2, 0, NT)
                 scale_store(i - 2, ALL, "G")
+            if h < B:
+                quantise_qk(i, Q)
         b = B - 1
         ev_p(b, K, ALL, "S")
         quantise_qk(b, K, 0, 2)

@@ -250,28 +250,31 @@ def tile_dynamicgraphattention_t_kernel(tc, H_t, A_stat, M_mask, Wq, Wk, out):
             h = i + 1
             key = "h%d" % h
             if h in parted:
-                fill_parted(key, parted[h], range(PARTED))
-                fill_t(key, h_raw[h], range(PARTED, NT))
+                fill_parted(key, parted[h], (0, 1))
             elif h < B:
-                fill_t(key, h_raw[h], ALL)
+                fill_t(key, h_raw[h], (0, 1))
             ev_p(i - 1, K, ALL, "S")
             quantise_qk(i - 1, K)
             fill_p(i, Q, ALL)
             if h < B:
                 h_op[h] = operand_tiles("h", 2)
-                ev_t(key, h_op[h], (1, 0), "S")
-                ev_t(key, h_op[h], (3, 2), "V")
+                ev_t(key, h_op[h], (0, 1), "S")
                 if h + 1 < B:
                     parted[h + 1] = part_words(h_raw[h + 1])
-                quantise_blocks(h_op[h], 0, 2)
-            fill_s(i - 1, ALL)
+                if h in parted:
+                    fill_parted(key, parted[h], (2,))
+                    fill_t(key, h_raw[h], (3,))
+                else:
+                    fill_t(key, h_raw[h], (2, 3))
+                ev_t(key, h_op[h], (2, 3), "V")
             ev_p(i, Q, ALL, "S")
+            fill_s(i - 1, ALL)
             fill_p(i, K, ALL)
             if i >= 2:
                 exps(i - 2, ALL)
             add_bias(i - 1, ALL)
             if h < B:
-                quantise_blocks(h_op[h], 2, 4)
+                quantise_blocks(h_op[h], 0, 4)
                 row_min(i - 1, 0, NT)
             else:
                 quantise_qk(i, Q)

@@ -212,6 +212,8 @@ def tile_dynamicgraphattention_t_kernel(tc, H_t, A_stat, M_mask, Wq, Wk, out):
                 e = probs[b][:, i, :]
                 if eng == "V":
                     nc.vector.tensor_scalar(out=e, in0=e, scalar1=rs[:, i:i + 1], scalar2=None, op0=ALU.mult)
+                elif eng == "S":
+                    nc.scalar.activation(out=e, in_=e, func=ACT.Copy, scale=rs[:, i:i + 1])
                 else:
                     nc.gpsimd.tensor_scalar(out=e, in0=e, scalar1=rs[:, i:i + 1], scalar2=1.0, op0=ALU.mult, op1=ALU.mult)
                 nc.sync.dma_start(out=out[b, i * P:(i + 1) * P, :], in_=e)
@@ -234,16 +236,19 @@ def tile_dynamicgraphattention_t_kernel(tc, H_t, A_stat, M_mask, Wq, Wk, out):
         ev_t("wk", w_op[K], (0, 1), "S")
         ev_t("wk", w_op[K], (3, 2), "V")
         quantise_blocks(w_op[K], 0, 4)
-        fill_p(0, Q, ALL)
         h_op[1] = operand_tiles("h", 2)
-        fill_t("h1", h_raw[1], ALL)
-        ev_p(0, Q, ALL, "S")
-        ev_t("h1", h_op[1], (1, 0), "S")
-        ev_t("h1", h_op[1], (3, 2), "V")
-        quantise_blocks(h_op[1], 0, 4)
-        parted = {}
+        fill_p(0, Q, (0, 1))
+        fill_t("h1", h_raw[1], (0, 1))
+        ev_p(0, Q, (0, 1), "S")
+        fill_p(0, Q, (2, 3))
+        ev_t("h1", h_op[1], (0, 1), "V")
+        fill_t("h1", h_raw[1], (2, 3))
+        ev_p(0, Q, (2, 3), "S")
+        ev_t("h1", h_op[1], (2, 3), "V")
         fill_p(0, K, ALL)
         quantise_qk(0, Q)
+        quantise_blocks(h_op[1], 0, 4)
+        parted = {}
         make_bias()
 
         for i in range(1, B):
@@ -268,11 +273,12 @@ def tile_dynamicgraphattention_t_kernel(tc, H_t, A_stat, M_mask, Wq, Wk, out):
                     fill_t(key, h_raw[h], (2, 3))
                 ev_t(key, h_op[h], (2, 3), "V")
             ev_p(i, Q, ALL, "S")
-            fill_s(i - 1, ALL)
+            tiles = ALL if h < B else (0, 1, 2)
+            fill_s(i - 1, tiles)
             fill_p(i, K, ALL)
             if i >= 2:
                 exps(i - 2, ALL)
-            add_bias(i - 1, ALL)
+            add_bias(i - 1, tiles)
             if h < B:
                 quantise_blocks(h_op[h], 0, 4)
                 row_min(i - 1, 0, NT)
@@ -286,22 +292,32 @@ def tile_dynamicgraphattention_t_kernel(tc, H_t, A_stat, M_mask, Wq, Wk, out):
                 quantise_qk(i, Q)
         b = B - 1
         ev_p(b, K, ALL, "S")
+        fill_s(b - 1, (3,))
         quantise_qk(b, K, 0, 2)
         quantise_qk(b, K, 2, 4)
-        row_min(b - 1, 2, NT)
+        add_bias(b - 1, (3,))
+        row_min(b - 1, 2, 3)
+        row_min(b - 1, 3, 4)
         fill_s(b, ALL)
         exps(b - 1, ALL)
-        for i in range(NT):
-            add_bias(b, (i,))
-            if i > 0:
-                row_min(b, i - 1, i)
-                exps(b, (i - 1,))
-            if i == 1:
-                recip(b - 1, 0, NT)
-                scale_store(b - 1, ALL, "G")
+        add_bias(b, (0, 1))
+        row_min(b, 0, 1)
+        exps(b, (0,))
+        add_bias(b, (2,))
+        recip(b - 1, 0, NT)
+        scale_store(b - 1, (0, 1), "G")
+        scale_store(b - 1, (2,), "S")
+        row_min(b, 1, 2)
+        exps(b, (1,))
+        add_bias(b, (3,))
+        scale_store(b - 1, (3,), "S")
+        row_min(b, 2, 3)
+        exps(b, (2,))
+        recip(b, 0, 2)
+        scale_store(b, (0, 1), "G")
         row_min(b, 3, 4)
         exps(b, (3,))
-        recip(b, 0, 3)
-        scale_store(b, (0, 1, 2), "V")
+        recip(b, 2, 3)
+        scale_store(b, (2,), "V")
         recip(b, 3, 4)
         scale_store(b, (3,), "V")

from contextlib import ExitStack

import concourse.mybir as mybir
from concourse.masks import make_identity

F32 = mybir.dt.float32
BF16 = mybir.dt.bfloat16
U32 = mybir.dt.uint32
U8 = mybir.dt.uint8
FP8X4 = mybir.dt.float8_e4m3fn_x4
ALU = mybir.AluOpType
ACT = mybir.ActivationFunctionType
AX = mybir.AxisListType

B, N, C, D = 8, 512, 1024, 512
P = 128
NT = N // P
FLOPS = 2 * (2 * B * N * C * D) + 2 * B * N * N * D
SCALE = 0.5 / (1.5 * 32.0)
BIG = 1.0e38
Q, K = 0, 1
BANKS = 8
ALL = (0, 1, 2, 3)
PARTED = 3


def tile_dynamicgraphattention_t_kernel(tc, H_t, A_stat, M_mask, Wq, Wk, out):
    nc = tc.nc
    with ExitStack() as ctx:
        const = ctx.enter_context(tc.tile_pool(name="const", bufs=1))
        raw = ctx.enter_context(tc.tile_pool(name="raw", bufs=1))
        mx = ctx.enter_context(tc.tile_pool(name="mx", bufs=2))
        work = ctx.enter_context(tc.tile_pool(name="work", bufs=3))
        perm = ctx.enter_context(tc.tile_pool(name="perm", bufs=2))
        small = ctx.enter_context(tc.tile_pool(name="small", bufs=4))
        psum = ctx.enter_context(tc.psum_pool(name="psum", bufs=1))
        ctx.enter_context(tc.manual_schedule())

        fills = {"n": 0}

        def new_bank():
            k = fills["n"] % BANKS
            fills["n"] += 1
            bank = psum.tile([P, 512], F32, name="bank%d" % k, tag="bank%d" % k)
            return bank

        def copy_out(eng, dst, src):
            if eng == "V":
                nc.vector.tensor_copy(out=dst, in_=src)
            else:
                nc.scalar.copy(out=dst, in_=src)

        ident = const.tile([P, P], F32, name="ident")
        make_identity(nc, ident[:])
        one = const.tile([P, 1], F32, name="one")
        nc.vector.memset(one[:], 0.0)
        warm = const.tile([P, 1], F32, name="warm")
        nc.scalar.activation(out=warm[:], in_=one[:], func=ACT.Exp)
        pen_diag = const.tile([P, 1, P], BF16, name="pen_diag")
        nc.vector.tensor_scalar(out=pen_diag[:, 0, :], in0=ident[:], scalar1=-2.0 * BIG, scalar2=BIG, op0=ALU.mult, op1=ALU.add)

        w_raw = [raw.tile([P, 4, C], BF16, name="w_raw%d" % x) for x in range(2)]
        h_raw = [raw.tile([P, NT, C], BF16, name="h_raw%d" % b) for b in range(B)]
        m_sb = const.tile([P, NT, N], BF16, name="m_sb")
        a_sb = const.tile([P, NT, N], BF16, name="a_sb")
        w_pen = const.tile([P, NT, N], BF16, name="w_pen")
        bias = const.tile([P, NT * (N + P)], BF16, name="bias")
        wq_v = Wq.rearrange("(p t) c -> p t c", t=4)
        wk_v = Wk.rearrange("(p t) c -> p t c", t=4)
        for t in range(4):
            nc.sync.dma_start(out=w_raw[Q][:, t, :], in_=wq_v[:, t, :])
        for j in range(NT):
            nc.sync.dma_start(out=h_raw[0][:, j, :], in_=H_t[0, j * P:(j + 1) * P, :])
        for t in range(4):
            nc.sync.dma_start(out=w_raw[K][:, t, :], in_=wk_v[:, t, :])
        for b in range(1, B):
            nc.sync.dma_start(out=h_raw[b][:], in_=H_t[b].rearrange("(j p) c -> p j c", p=P))
            if b == 2:
                nc.sync.dma_start(out=m_sb[:], in_=M_mask.rearrange("(i p) m -> p i m", p=P))
                nc.sync.dma_start(out=a_sb[:], in_=A_stat.rearrange("(i p) m -> p i m", p=P))

        def operand_tiles(tag, bufs):
            g = mx.tile([P, 4, 2, P, 4], BF16, name=tag + "_g", tag=tag + "_g", bufs=bufs, align_bytes=64)
            c = mx.tile([P, 4, 2, P], U32, name=tag + "_c", tag=tag + "_c", bufs=bufs, align_bytes=64)
            s = mx.tile([P, 4, 2, P], U8, name=tag + "_s", tag=tag + "_s", bufs=bufs, align_bytes=64)
            return g, c, s

        banks = {}
        w_op = [operand_tiles("w%d" % x, 1) for x in range(2)]
        h_op = {}
        qk = {}
        nlog = {}
        mins = {}
        sums = {}
        recs = {}
        probs = {}

        def fill_t(key, src, js):
            words = src[:].bitcast(F32)
            for j in js:
                bank = new_bank()
                banks[(key, j)] = bank
                for g in range(2):
                    for u in range(2):
                        x = 2 * g + u
                        nc.tensor.transpose(bank[:, x * P:(x + 1) * P], words[:, j, 2 * P * g + u:2 * P * (g + 1):2], ident[:])

        def part_words(src):
            dst = perm.tile([P, 2, PARTED, 2 * P], F32, name="parted", tag="parted")
            nc.vector.tensor_copy(out=dst[:].rearrange("p u j w -> p u (j w)"), in_=src[:, 0:PARTED, :].rearrange("p j c -> p (j c)").bitcast(F32).rearrange("p (w u) -> p u w", u=2))
            return dst

        def fill_parted(key, dst, js):
            for j in js:
                bank = new_bank()
                banks[(key, j)] = bank
                for g in range(2):
                    for u in range(2):
                        x = 2 * g + u
                        nc.tensor.transpose(bank[:, x * P:(x + 1) * P], dst[:, u, j, g * P:(g + 1) * P], ident[:])

        def ev_t(key, opnd, js, eng):
            for j in js:
                copy_out(eng, opnd[0][:].bitcast(F32)[:, j], banks[(key, j)][:].rearrange("q (g u n) -> q g n u", g=2, u=2))

        def quantise_blocks(opnd, j0, j1):
            g, c, s = opnd
            nc.vector.quantize_mx(
                out=c[:, j0:j1].rearrange("p j g n -> p (j g n)").bitcast(FP8X4),
                scales=s[:, j0:j1].rearrange("p j g n -> p (j g n)"),
                in_=g[:, j0:j1].rearrange("p j g n f -> p (j g n f)"),
            )

        def fill_p(b, x, js):
            if b not in qk:
                qk[b] = (
                    mx.tile([P, 2, N, 4], BF16, name="qk_g", tag="qk_g", align_bytes=64),
                    mx.tile([P, 2, N], U32, name="qk_c", tag="qk_c", align_bytes=64),
                    mx.tile([P, 2, N], U8, name="qk_s", tag="qk_s", align_bytes=64),
                )
            hc, hs = h_op[b][1], h_op[b][2]
            wc, ws = w_op[x][1], w_op[x][2]
            for j in js:
                bank = new_bank()
                banks[("p", b, x, j)] = bank
                for t in range(4):
                    for g in range(2):
                        nc.tensor.matmul_mx(
                            out=bank[:, t * P:(t + 1) * P],
                            lhsT=wc[:, t, g, :].bitcast(FP8X4), lhsT_scale=ws[:, t, g, :],
                            rhs=hc[:, j, g, :].bitcast(FP8X4), rhs_scale=hs[:, j, g, :],
                            start=(g == 0), stop=(g == 1),
                        )

        def ev_p(b, x, js, eng):
            for j in js:
                copy_out(eng, qk[b][0][:, x, j * P:(j + 1) * P, :], banks[("p", b, x, j)][:].rearrange("m (t n) -> m n t", t=4))

        def quantise_qk(b, x, j0=0, j1=NT):
            g, c, s = qk[b]
            n = slice(j0 * P, j1 * P)
            nc.vector.quantize_mx(out=c[:, x, n].bitcast(FP8X4), scales=s[:, x, n], in_=g[:, x, n].rearrange("p n t -> p (n t)"))

        def fill_s(b, tiles):
            c, s = qk[b][1], qk[b][2]
            for i in tiles:
                bank = new_bank()
                banks[("s", b, i)] = bank
                rows = slice(i * P, (i + 1) * P)
                for x in range(2):
                    nc.tensor.matmul_mx(
                        out=bank[:],
                        lhsT=c[:, x, rows].bitcast(FP8X4), lhsT_scale=s[:, x, rows],
                        rhs=c[:, 1 - x, :].bitcast(FP8X4), rhs_scale=s[:, 1 - x, :],
                        start=(x == 0), stop=(x == 1),
                    )

        bias_v = bias[:, 0:NT * N].rearrange("p (i m) -> p i m", i=NT)

        def make_bias():
            nc.vector.tensor_scalar(out=w_pen[:], in0=m_sb[:], scalar1=0.0, scalar2=2.0 * BIG, op0=ALU.is_gt, op1=ALU.mult)
            nc.vector.tensor_scalar(out=w_pen[:], in0=w_pen[:], scalar1=BIG, scalar2=None, op0=ALU.subtract)
            nc.vector.tensor_tensor(out=bias_v, in0=w_pen[:], in1=a_sb[:], op=ALU.min)
            blk = bias[:].rearrange("p (i m) -> p i m", i=NT)[:, :, 0:P]
            nc.vector.tensor_tensor(out=blk, in0=blk, in1=pen_diag[:].to_broadcast([P, NT, P]), op=ALU.min)

        def add_bias(b, tiles):
            if b not in nlog:
                nlog[b] = work.tile([P, NT, N], F32, name="nlog", tag="nlog", bufs=2)
                mins[b] = small.tile([P, NT], F32, name="mins", tag="mins")
            for i in tiles:
                nc.vector.scalar_tensor_tensor(out=nlog[b][:, i, :], in0=banks[("s", b, i)][:], scalar=-SCALE, in1=bias_v[:, i, :], op0=ALU.mult, op1=ALU.subtract)

        def row_min(b, i0, i1):
            nc.vector.tensor_reduce(out=mins[b][:, i0:i1], in_=nlog[b][:, i0:i1, :], axis=AX.X, op=ALU.min)

        def exps(b, tiles):
            if b not in probs:
                probs[b] = work.tile([P, NT, N], F32, name="probs", tag="probs")
                sums[b] = small.tile([P, NT], F32, name="sums", tag="sums")
            for i in tiles:
                nc.scalar.activation(out=probs[b][:, i, :], in_=nlog[b][:, i, :], func=ACT.Exp, bias=mins[b][:, i:i + 1], scale=-1.0, accum_out=sums[b][:, i:i + 1])

        def recip(b, lo, hi):
            if b not in recs:
                recs[b] = small.tile([P, NT], F32, name="rs", tag="rs")
            nc.vector.reciprocal(out=recs[b][:, lo:hi], in_=sums[b][:, lo:hi])

        def scale_store(b, tiles, eng):
            rs = recs[b]
            for i in tiles:
                e = probs[b][:, i, :]
                if eng == "V":
                    nc.vector.tensor_scalar(out=e, in0=e, scalar1=rs[:, i:i + 1], scalar2=None, op0=ALU.mult)
                elif eng == "S":
                    nc.scalar.activation(out=e, in_=e, func=ACT.Copy, scale=rs[:, i:i + 1])
                else:
                    nc.gpsimd.tensor_scalar(out=e, in0=e, scalar1=rs[:, i:i + 1], scalar2=1.0, op0=ALU.mult, op1=ALU.mult)
                nc.sync.dma_start(out=out[b, i * P:(i + 1) * P, :], in_=e)

        for t in range(4):
            fill_t("wq", w_raw[Q], (t,))
            ev_t("wq", w_op[Q], (t,), "S")
            if t > 0:
                quantise_blocks(w_op[Q], t - 1, t)
        h_op[0] = operand_tiles("h", 2)
        for j in range(NT):
            fill_t("h0", h_raw[0], (j,))
            ev_t("h0", h_op[0], (j,), "S")
            if j == 0:
                quantise_blocks(w_op[Q], 3, 4)
            else:
                quantise_blocks(h_op[0], j - 1, j)
        quantise_blocks(h_op[0], 3, 4)
        fill_t("wk", w_raw[K], ALL)
        ev_t("wk", w_op[K], (0, 1), "S")
        ev_t("wk", w_op[K], (3, 2), "V")
        quantise_blocks(w_op[K], 0, 4)
        h_op[1] = operand_tiles("h", 2)
        fill_p(0, Q, (0, 1))
        fill_t("h1", h_raw[1], (0, 1))
        ev_p(0, Q, (0, 1), "S")
        fill_p(0, Q, (2, 3))
        ev_t("h1", h_op[1], (0, 1), "V")
        fill_t("h1", h_raw[1], (2, 3))
        ev_p(0, Q, (2, 3), "S")
        ev_t("h1", h_op[1], (2, 3), "V")
        fill_p(0, K, ALL)
        quantise_qk(0, Q)
        quantise_blocks(h_op[1], 0, 4)
        parted = {}
        make_bias()

        for i in range(1, B):
            h = i + 1
            key = "h%d" % h
            if h in parted:
                fill_parted(key, parted[h], (0, 1))
            elif h < B:
                fill_t(key, h_raw[h], (0, 1))
            ev_p(i - 1, K, ALL, "S")
            quantise_qk(i - 1, K)
            fill_p(i, Q, ALL)
            if h < B:
                h_op[h] = operand_tiles("h", 2)
                ev_t(key, h_op[h], (0, 1), "S")
                if h + 1 < B:
                    parted[h + 1] = part_words(h_raw[h + 1])
                if h in parted:
                    fill_parted(key, parted[h], (2,))
                    fill_t(key, h_raw[h], (3,))
                else:
                    fill_t(key, h_raw[h], (2, 3))
                ev_t(key, h_op[h], (2, 3), "V")
            ev_p(i, Q, ALL, "S")
            tiles = ALL if h < B else (0, 1, 2)
            fill_s(i - 1, tiles)
            fill_p(i, K, ALL)
            if i >= 2:
                exps(i - 2, ALL)
            add_bias(i - 1, tiles)
            if h < B:
                quantise_blocks(h_op[h], 0, 4)
                row_min(i - 1, 0, NT)
            else:
                quantise_qk(i, Q)
                row_min(i - 1, 0, 2)
            if i >= 2:
                recip(i - 2, 0, NT)
                scale_store(i - 2, ALL, "G")
            if h < B:
                quantise_qk(i, Q)
        b = B - 1
        ev_p(b, K, ALL, "S")
        fill_s(b - 1, (3,))
        quantise_qk(b, K, 0, 2)
        quantise_qk(b, K, 2, 4)
        add_bias(b - 1, (3,))
        row_min(b - 1, 2, 3)
        row_min(b - 1, 3, 4)
        fill_s(b, ALL)
        exps(b - 1, ALL)
        add_bias(b, (0, 1))
        row_min(b, 0, 1)
        exps(b, (0,))
        add_bias(b, (2,))
        recip(b - 1, 0, NT)
        scale_store(b - 1, (0, 1), "G")
        scale_store(b - 1, (2,), "S")
        row_min(b, 1, 2)
        exps(b, (1,))
        add_bias(b, (3,))
        scale_store(b - 1, (3,), "S")
        row_min(b, 2, 3)
        exps(b, (2,))
        recip(b, 0, 2)
        scale_store(b, (0, 1), "G")
        row_min(b, 3, 4)
        exps(b, (3,))
        recip(b, 2, 3)
        scale_store(b, (2,), "V")
        recip(b, 3, 4)
        scale_store(b, (3,), "V")
